import numpy as np
import ml_dtypes


def mxq(x, axis, fmt="e4m3"):
    dtype, down = {"e4m3": (ml_dtypes.float8_e4m3fn, 7), "e5m2": (ml_dtypes.float8_e5m2, 14)}[fmt]
    v = np.moveaxis(np.asarray(x, np.float32).astype(ml_dtypes.bfloat16).astype(np.float64), axis, -1)
    blocks = v.reshape(v.shape[:-1] + (-1, 32))
    amax = np.abs(blocks).max(-1, keepdims=True)
    byte = np.maximum(np.where(amax > 0, np.frexp(amax)[1] - 1 + 127, 0) - down, 1)
    scale = np.exp2(byte - 127.0)
    codes = (blocks / scale).astype(np.float32).astype(dtype).astype(np.float64)
    return np.moveaxis((codes * scale).reshape(v.shape), -1, axis)


WIDE = False


def mx_kscale(k):
    if not WIDE:
        return np.ones(k)
    levels = np.array([10, -10, 5, -5, 0])
    if k % 512:
        return np.exp2(np.random.permutation(np.resize(levels, k // 32))).repeat(32)
    a = np.empty((k // 512, 16))
    for p in range(k // 512):
        a[p, :8] = np.random.permutation(np.resize(levels, 8))
        for g in range(8):
            far = levels[np.abs(levels - a[p, g]) >= 10]
            a[p, g + 8] = far[np.random.randint(len(far))]
    return np.exp2(a.ravel()).repeat(32)


BF16 = ml_dtypes.bfloat16


def bf(x):
    return np.asarray(x, np.float32).astype(BF16)


def f64(x):
    return np.asarray(x).astype(np.float64)


N, C0, H, KS, P, C, O, F, NC = 512, 1, 4, 3, 2, 512, 512, 512, 10
KK = KS * KS
OH = H - KS + 1
OP = OH // P
FC = O * OP * OP


def relu(v):
    return np.maximum(v, 0.0)


def maxpool(v):
    n, c, hh, ww = v.shape
    hp, wp = hh // P, ww // P
    return v[:, :, :hp * P, :wp * P].reshape(n, c, hp, P, wp, P).max(axis=(3, 5))


def draw0():
    s = mx_kscale(C)
    t = mx_kscale(FC)
    tt = np.repeat(np.repeat(t.reshape(O, OP, OP), P, axis=1), P, axis=2)
    h = np.maximum(np.random.standard_normal((P * P, N, C, H, H)).max(0), 0.0)
    return {
        "h_pool1": bf(h * s[None, :, None, None]),
        "w2": bf(np.random.standard_normal((O, C, KK, OH, OH)) * 0.8 / np.sqrt(KK * C) / s[None, :, None, None, None] * tt[:, None, None, :, :]),
        "b2": bf(np.random.standard_normal((O, OH, OH)) * 0.3 * tt),
        "fc1_w": bf(np.random.standard_normal((FC, F)) * 0.8 / np.sqrt(FC) / t[:, None]),
        "fc1_b": bf(np.random.standard_normal(F) * 0.3),
    }


def core(h_pool1, w2, b2, fc1_w, fc1_b):
    hq = mxq(f64(h_pool1).transpose(2, 3, 0, 1), 3, "e4m3")
    wq = mxq(f64(w2).transpose(2, 3, 4, 1, 0), 3, "e4m3")
    y = sum((hq[i:i + OH, j:j + OH] @ wq[i * KS + j]) for i in range(KS) for j in range(KS))
    y = y.transpose(2, 3, 0, 1) + f64(b2)
    g = maxpool(relu(y)).reshape(N, FC)
    return relu((mxq(g, 1, "e4m3") @ mxq(f64(fc1_w), 0, "e4m3")) + f64(fc1_b))


def e4m3fn_bytes(y):
    return np.clip(np.asarray(y, np.float64), -448.0, 448.0).astype(np.float32).astype(ml_dtypes.float8_e4m3fn).view(np.uint8)


def e4m3fn_values(b):
    return np.asarray(b, np.uint8).view(ml_dtypes.float8_e4m3fn).astype(np.float64)


def setup_inputs():
    d = draw0()
    x0 = np.asarray(d['h_pool1']).astype(np.float64)
    s = (np.max(np.abs(x0), axis=(0, 2, 3), keepdims=True) / 448.0).astype(np.float32)
    out = {}
    for k, v in d.items():
        if k == 'h_pool1':
            out['h_pool1_bytes'] = e4m3fn_bytes(x0 / s.astype(np.float64))
            out['h_pool1_scale'] = s
        else:
            out[k] = v
    return out


def reference(h_pool1_bytes, h_pool1_scale, w2, b2, fc1_w, fc1_b):
    return core(e4m3fn_values(h_pool1_bytes) * h_pool1_scale.astype(np.float64), w2, b2, fc1_w, fc1_b)

@@ -1,0 +1,289 @@
+from contextlib import ExitStack
+
+import concourse.mybir as mybir
+from concourse.masks import make_identity
+
+F32 = mybir.dt.float32
+BF16 = mybir.dt.bfloat16
+U32 = mybir.dt.uint32
+U8 = mybir.dt.uint8
+FP8 = mybir.dt.float8_e4m3fn
+FP8X4 = mybir.dt.float8_e4m3fn_x4
+ALU = mybir.AluOpType
+ACT = mybir.ActivationFunctionType
+
+P = 128
+NB = 512
+C = 512
+F = 512
+T = 4
+G = NB // P
+U = 4
+KK = 9
+POS = 4
+Q = KK * POS
+PIX = 16
+HALF = 64
+
+FLOPS = 37 * 2 * 512 * 512 * 512
+
+
+def tile_locallyconnectednet_pa_t_kernel(tc, h_bytes, h_scale, w2, b2, fc1_w, fc1_b, out):
+    nc = tc.nc
+    with ExitStack() as ctx:
+        keep = ctx.enter_context(tc.tile_pool(name="keep", bufs=1))
+        bytes_pool = ctx.enter_context(tc.tile_pool(name="bytes_pool", bufs=4))
+        wide_pool = ctx.enter_context(tc.tile_pool(name="wide_pool", bufs=2))
+        group_pool = ctx.enter_context(tc.tile_pool(name="group_pool", bufs=5))
+        raw_pool = ctx.enter_context(tc.tile_pool(name="raw_pool", bufs=4))
+        code_pool = ctx.enter_context(tc.tile_pool(name="code_pool", bufs=2))
+        max_pool = ctx.enter_context(tc.tile_pool(name="max_pool", bufs=2))
+        psum_t = ctx.enter_context(tc.psum_pool(name="psum_t", bufs=4))
+        psum_a = ctx.enter_context(tc.psum_pool(name="psum_a", bufs=4))
+
+        ident = keep.tile([P, P], BF16)
+        make_identity(nc, ident[:])
+        ctx.enter_context(tc.manual_schedule())
+
+        hb = h_bytes.rearrange("(g n) c a b -> g n (c a b)", n=P)
+        wv = w2.rearrange("(m u) (p t) k i j -> u p m (t k i j)", u=U, t=T)
+        h_codes = keep.tile([P, PIX, NB], U32, align_bytes=64)
+        h_scales = keep.tile([P, PIX, NB], U8, align_bytes=64)
+        pooled = keep.tile([P, U, NB], BF16)
+        scale = keep.tile([P, T], F32)
+        scale_b = scale[:].unsqueeze(1).unsqueeze(1).to_broadcast([P, 2, P, T])
+        bias = keep.tile([P, U * POS], BF16)
+        fc_bias = keep.tile([P, F], BF16)
+        fc_codes = keep.tile([P, F], U32, align_bytes=64)
+        fc_scales = keep.tile([P, F], U8, align_bytes=64)
+        g_codes = keep.tile([P, NB], U32, align_bytes=64)
+        g_scales = keep.tile([P, NB], U8, align_bytes=64)
+
+        bytes_tiles = {}
+        raws = {}
+        wides = {}
+        groups = {}
+        w_codes = {}
+        w_scales = {}
+        accs = {}
+        best = {}
+
+        def group_tile(shape, dtype):
+            return group_pool.tile(shape, dtype, align_bytes=64, name="grouped")
+
+        def load_h(g, half):
+            raw_bytes = bytes_pool.tile([P, C * PIX // 2], U8, name="raw_bytes")
+            nc.sync.dma_start(out=raw_bytes[:], in_=hb[g][:, half * 4096 : half * 4096 + 4096])
+            bytes_tiles[g, half] = raw_bytes
+
+        def load_raw(u, half):
+            raw = raw_pool.tile([P, HALF, T * Q], BF16, name="raw")
+            for s in range(0, HALF, 32):
+                nc.sync.dma_start(out=raw[:, s : s + 32, :], in_=wv[u][:, half * HALF + s : half * HALF + s + 32, :])
+            raws[u, half] = raw
+
+        def widen(copy, g, half, lo, hi):
+            if g not in wides:
+                wides[g] = wide_pool.tile([P, C * PIX], BF16, name="wide")
+            copy(out=wides[g][:, half * 4096 + lo : half * 4096 + hi], in_=bytes_tiles[g, half][:, lo:hi].bitcast(FP8))
+
+        def h_turn(s):
+            g, x = s // 4, 4 * (s % 4)
+            for y in range(0, 4, 2):
+                turned = psum_t.tile([P, 2, T, P], BF16, name="turned")
+                for z in range(2):
+                    for t in range(T):
+                        nc.tensor.transpose(turned[:, z, t, :], wides[g][:, t * PIX + x + y + z :: T * PIX], ident[:])
+                groups["turned", s, y] = turned
+
+        def h_scale_step(s):
+            grouped = group_tile([P, 4, P, T], BF16)
+            for y in range(0, 4, 2):
+                nc.vector.tensor_tensor(
+                    out=grouped[:, y : y + 2],
+                    in0=groups["turned", s, y][:].rearrange("p z t n -> p z n t"),
+                    in1=scale_b,
+                    op=ALU.mult,
+                )
+            groups["h", s] = grouped
+
+        def h_quantise(s):
+            g, x = s // 4, 4 * (s % 4)
+            for y in range(4):
+                nc.vector.quantize_mx(
+                    out=h_codes[:, x + y, g * P : (g + 1) * P].bitcast(FP8X4),
+                    scales=h_scales[:, x + y, g * P : (g + 1) * P],
+                    in_=groups["h", s][:, y].rearrange("p n t -> p (n t)"),
+                )
+
+        def regroup(copy, u, k, half):
+            if (u, k) not in groups:
+                groups[u, k] = group_tile([P, POS, P, T], BF16)
+            copy(
+                out=groups[u, k][:, :, half * HALF : (half + 1) * HALF, :].rearrange("p q m t -> p (m t) q"),
+                in_=raws[u, half][:].rearrange("p m (t q) -> p (m t) q", t=T)[:, :, POS * k : POS * k + POS],
+            )
+
+        def w_quantise(u, k):
+            if k == 0:
+                w_codes[u] = code_pool.tile([P, KK, POS, P], U32, align_bytes=64, name="w_codes")
+                w_scales[u] = code_pool.tile([P, KK, POS, P], U8, align_bytes=64, name="w_scales")
+            nc.vector.quantize_mx(
+                out=w_codes[u][:, k].rearrange("p q m -> p (q m)").bitcast(FP8X4),
+                scales=w_scales[u][:, k].rearrange("p q m -> p (q m)"),
+                in_=groups[u, k][:].rearrange("p q m t -> p (q m t)"),
+            )
+
+        def products(u, k, lo, hi):
+            for q in range(POS):
+                if (u, q) not in accs:
+                    if u % 2:
+                        accs[u, q] = psum_t.tile([P, NB], F32, name="turned")
+                    else:
+                        accs[u, q] = psum_a.tile([P, NB], F32, name="acc")
+                i, j = q // 2, q % 2
+                pix = (k // 3 + i) * 4 + k % 3 + j
+                nc.tensor.matmul_mx(
+                    out=accs[u, q][:, lo:hi],
+                    lhsT=w_codes[u][:, k, q, :].bitcast(FP8X4),
+                    lhsT_scale=w_scales[u][:, k, q, :],
+                    rhs=h_codes[:, pix, lo:hi].bitcast(FP8X4),
+                    rhs_scale=h_scales[:, pix, lo:hi],
+                    start=(k == 0),
+                    stop=(k == KK - 1),
+                )
+
+        def pool_max(u, q):
+            b = bias[:, POS * u + q : POS * u + q + 1]
+            old = best.get(u)
+            if q < POS - 1:
+                best[u] = max_pool.tile([P, NB], F32, name="best")
+            if q == 0:
+                nc.scalar.activation(best[u][:], accs[u, q][:], ACT.Relu, bias=b)
+            else:
+                dst = best[u][:] if q < POS - 1 else pooled[:, u, :]
+                nc.vector.scalar_tensor_tensor(out=dst, in0=accs[u, q][:], scalar=b, in1=old[:], op0=ALU.add, op1=ALU.max)
+
+        fc_raw = group_tile([P, T, F], BF16)
+        nc.sync.dma_start(out=fc_raw[:], in_=fc1_w.rearrange("(p t) f -> p t f", t=T))
+        load_h(0, 0)
+        load_h(0, 1)
+        nc.sync.dma_start(out=scale[:], in_=h_scale.rearrange("o (p t) a b -> p (o t a b)", t=T))
+        load_h(1, 0)
+        load_h(1, 1)
+        load_raw(0, 0)
+        fc_grouped = group_tile([P, F, T], BF16)
+        nc.vector.tensor_copy(out=fc_grouped[:], in_=fc_raw[:].rearrange("p t f -> p f t"))
+        widen(nc.scalar.copy, 0, 0, 0, 2048)
+        widen(nc.vector.tensor_copy, 0, 0, 2048, 4096)
+        nc.vector.quantize_mx(out=fc_codes[:].bitcast(FP8X4), scales=fc_scales[:], in_=fc_grouped[:].rearrange("p f t -> p (f t)"))
+        widen(nc.vector.tensor_copy, 0, 1, 0, 4096)
+        load_h(2, 0)
+        load_h(2, 1)
+        load_raw(0, 1)
+        for half in range(2):
+            widen(nc.scalar.copy, 1, half, 0, 4096)
+        load_h(3, 0)
+        load_h(3, 1)
+        load_raw(1, 0)
+        load_raw(1, 1)
+        nc.sync.dma_start(out=fc_bias[:], in_=fc1_b.partition_broadcast(P))
+        nc.sync.dma_start(out=bias[:], in_=b2.rearrange("(p u) i j -> p (u i j)", u=U))
+
+        h_turn(0)
+        for s in range(16):
+            if s < 15:
+                h_turn(s + 1)
+            h_scale_step(s)
+            if s > 0:
+                h_quantise(s - 1)
+            if s in (3, 7):
+                g = 2 + s // 4
+                for half in range(2):
+                    widen(nc.scalar.copy, g, half, 0, 4096)
+            if s in (4, 7, 8, 9, 10, 11, 12, 13, 14):
+                k = (4, 7, 8, 9, 10, 11, 12, 13, 14).index(s)
+                for half in range(2):
+                    regroup(nc.scalar.copy, 0, k, half)
+            if s in (8, 10, 11, 12, 13, 14, 15):
+                k = (8, 10, 11, 12, 13, 14, 15).index(s)
+                w_quantise(0, k)
+                if s == 10:
+                    products(0, 0, 0, 256)
+                if s >= 10:
+                    products(0, k, 0, 256)
+        load_raw(2, 0)
+        load_raw(2, 1)
+        h_quantise(15)
+
+        for k in (7, 8):
+            w_quantise(0, k)
+            products(0, k, 0, 256)
+        for k in range(KK):
+            products(0, k, 256, 512)
+        units = [(u, k) for u in range(1, U) for k in range(KK)]
+        for n, (u, k) in enumerate(units):
+            regroup(nc.scalar.copy, u, k, 0)
+            regroup(nc.scalar.copy if n % 5 == 5 - 1 else nc.vector.tensor_copy, u, k, 1)
+            if n > 0:
+                w_quantise(*units[n - 1])
+                products(*units[n - 1], 0, NB)
+            if k == KK - 1 and u + 2 < U:
+                load_raw(u + 2, 0)
+                load_raw(u + 2, 1)
+            if k in (2, 4, 5, 6):
+                pool_max(u - 1, (2, 4, 5, 6).index(k))
+        w_quantise(*units[-1])
+        products(*units[-1], 0, NB)
+        for q in range(POS):
+            pool_max(U - 1, q)
+
+        g_grouped = group_tile([P, NB, U], BF16)
+
+        def dense_group(g):
+            cols = slice(g * P, (g + 1) * P)
+            nc.vector.tensor_copy(out=g_grouped[:, cols, :], in_=pooled[:, :, cols].rearrange("p u n -> p n u"))
+
+        def dense_quantise(g):
+            cols = slice(g * P, (g + 1) * P)
+            nc.vector.quantize_mx(
+                out=g_codes[:, cols].bitcast(FP8X4), scales=g_scales[:, cols], in_=g_grouped[:, cols, :].rearrange("p n u -> p (n u)")
+            )
+
+        prods = {}
+
+        def dense_product(g):
+            cols = slice(g * P, (g + 1) * P)
+            prods[g] = psum_a.tile([P, F], F32, name="acc")
+            nc.tensor.matmul_mx(
+                out=prods[g][:],
+                lhsT=g_codes[:, cols].bitcast(FP8X4),
+                lhsT_scale=g_scales[:, cols],
+                rhs=fc_codes[:].bitcast(FP8X4),
+                rhs_scale=fc_scales[:],
+                start=True,
+                stop=True,
+            )
+
+        def dense_out(g):
+            cols = slice(g * P, (g + 1) * P)
+            total = group_tile([P, F], F32)
+            nc.vector.tensor_tensor(out=total[:], in0=prods[g][:], in1=fc_bias[:], op=ALU.add)
+            res = group_tile([P, F], F32)
+            nc.scalar.activation(res[:], total[:], ACT.Relu)
+            nc.sync.dma_start(out=out[cols, :], in_=res[:])
+
+        dense_group(0)
+        dense_group(1)
+        dense_quantise(0)
+        dense_product(0)
+        dense_group(2)
+        dense_quantise(1)
+        dense_product(1)
+        dense_group(3)
+        dense_quantise(2)
+        dense_product(2)
+        dense_quantise(3)
+        dense_product(3)
+        for g in range(G):
+            dense_out(g)

@@ -25,6 +25,11 @@ Q = KK * POS
 PIX = 16
 HALF = 64
 
+WIDE_AT = 73728
+BYTES_AT = WIDE_AT + 2 * 16384
+RAW_AT = {(1, 0): 36864, (1, 1): 55296, (2, 0): 145920, (2, 1): 96768, (3, 0): 0, (3, 1): 18432}
+CODES_AT = {0: 122880, 1: 73728, 2: 122880, 3: 73728}
+
 FLOPS = 37 * 2 * 512 * 512 * 512
 
 
@@ -32,13 +37,12 @@ def tile_locallyconnectednet_pa_t_kernel(tc, h_bytes, h_scale, w2, b2, fc1_w, fc
     nc = tc.nc
     with ExitStack() as ctx:
         keep = ctx.enter_context(tc.tile_pool(name="keep", bufs=1))
-        bytes_pool = ctx.enter_context(tc.tile_pool(name="bytes_pool", bufs=4))
-        wide_pool = ctx.enter_context(tc.tile_pool(name="wide_pool", bufs=2))
-        group_pool = ctx.enter_context(tc.tile_pool(name="group_pool", bufs=5))
-        raw_pool = ctx.enter_context(tc.tile_pool(name="raw_pool", bufs=4))
-        code_pool = ctx.enter_context(tc.tile_pool(name="code_pool", bufs=2))
+        space = ctx.enter_context(tc.tile_pool(name="space", bufs=1))
+        h_pool = ctx.enter_context(tc.tile_pool(name="h_pool", bufs=2))
+        w_pool = ctx.enter_context(tc.tile_pool(name="w_pool", bufs=3))
         max_pool = ctx.enter_context(tc.tile_pool(name="max_pool", bufs=2))
-        psum_t = ctx.enter_context(tc.psum_pool(name="psum_t", bufs=4))
+        psum_h = ctx.enter_context(tc.psum_pool(name="psum_h", bufs=2))
+        psum_w = ctx.enter_context(tc.psum_pool(name="psum_w", bufs=2))
         psum_a = ctx.enter_context(tc.psum_pool(name="psum_a", bufs=4))
 
         ident = keep.tile([P, P], BF16)
@@ -68,36 +72,46 @@ def tile_locallyconnectednet_pa_t_kernel(tc, h_bytes, h_scale, w2, b2, fc1_w, fc
         accs = {}
         best = {}
 
-        def group_tile(shape, dtype):
-            return group_pool.tile(shape, dtype, align_bytes=64, name="grouped")
+        def h_tile(shape, dtype):
+            return h_pool.tile(shape, dtype, align_bytes=64, name="h_grouped")
+
+        def w_tile(shape, dtype):
+            return w_pool.tile(shape, dtype, align_bytes=64, name="w_grouped")
+
+        def unit_tile(u, k):
+            if u > 0 and ((u - 1) * KK + k) % 5 > 2:
+                return h_tile([P, POS, P, T], BF16)
+            return w_tile([P, POS, P, T], BF16)
 
         def load_h(g, half):
-            raw_bytes = bytes_pool.tile([P, C * PIX // 2], U8, name="raw_bytes")
+            n = (2 * g + half) % 4
+            raw_bytes = space.tile([P, C * PIX // 2], U8, name="raw_bytes%d" % n, offset=BYTES_AT + 4096 * n)
             nc.sync.dma_start(out=raw_bytes[:], in_=hb[g][:, half * 4096 : half * 4096 + 4096])
             bytes_tiles[g, half] = raw_bytes
 
         def load_raw(u, half):
-            raw = raw_pool.tile([P, HALF, T * Q], BF16, name="raw")
+            at = RAW_AT[u, half]
+            raw = space.tile([P, HALF, T * Q], BF16, name="raw%d" % at, offset=at)
             for s in range(0, HALF, 32):
                 nc.sync.dma_start(out=raw[:, s : s + 32, :], in_=wv[u][:, half * HALF + s : half * HALF + s + 32, :])
             raws[u, half] = raw
 
         def widen(copy, g, half, lo, hi):
             if g not in wides:
-                wides[g] = wide_pool.tile([P, C * PIX], BF16, name="wide")
+                wides[g] = space.tile([P, C * PIX], BF16, name="wide%d" % (g % 2), offset=WIDE_AT + 16384 * (g % 2))
             copy(out=wides[g][:, half * 4096 + lo : half * 4096 + hi], in_=bytes_tiles[g, half][:, lo:hi].bitcast(FP8))
 
         def h_turn(s):
             g, x = s // 4, 4 * (s % 4)
             for y in range(0, 4, 2):
-                turned = psum_t.tile([P, 2, T, P], BF16, name="turned")
+                turned = psum_h.tile([P, 2, T, P], BF16, name="turned")
                 for z in range(2):
                     for t in range(T):
                         nc.tensor.transpose(turned[:, z, t, :], wides[g][:, t * PIX + x + y + z :: T * PIX], ident[:])
                 groups["turned", s, y] = turned
 
         def h_scale_step(s):
-            grouped = group_tile([P, 4, P, T], BF16)
+            grouped = h_tile([P, 4, P, T], BF16)
             for y in range(0, 4, 2):
                 nc.vector.tensor_tensor(
                     out=grouped[:, y : y + 2],
@@ -118,16 +132,26 @@ def tile_locallyconnectednet_pa_t_kernel(tc, h_bytes, h_scale, w2, b2, fc1_w, fc
 
         def regroup(copy, u, k, half):
             if (u, k) not in groups:
-                groups[u, k] = group_tile([P, POS, P, T], BF16)
+                groups[u, k] = unit_tile(u, k)
             copy(
                 out=groups[u, k][:, :, half * HALF : (half + 1) * HALF, :].rearrange("p q m t -> p (m t) q"),
                 in_=raws[u, half][:].rearrange("p m (t q) -> p (m t) q", t=T)[:, :, POS * k : POS * k + POS],
             )
 
+        def w_turn(u, k, y):
+            if (u, k) not in groups:
+                groups[u, k] = unit_tile(u, k)
+            turned = psum_w.tile([P, 2, T, P], BF16, name="w_turned")
+            for z in range(2):
+                for t in range(T):
+                    nc.tensor.transpose(turned[:, z, t, :], natural[:, t * Q + POS * k + y + z :: T * Q], ident[:])
+            nc.scalar.copy(out=groups[u, k][:, y : y + 2], in_=turned[:].rearrange("p z t m -> p z m t"))
+
         def w_quantise(u, k):
             if k == 0:
-                w_codes[u] = code_pool.tile([P, KK, POS, P], U32, align_bytes=64, name="w_codes")
-                w_scales[u] = code_pool.tile([P, KK, POS, P], U8, align_bytes=64, name="w_scales")
+                at = CODES_AT[u]
+                w_codes[u] = space.tile([P, KK, POS, P], U32, align_bytes=64, name="w_codes%d" % at, offset=at)
+                w_scales[u] = space.tile([P, KK, POS, P], U8, align_bytes=64, name="w_scales%d" % at, offset=at + 18432)
             nc.vector.quantize_mx(
                 out=w_codes[u][:, k].rearrange("p q m -> p (q m)").bitcast(FP8X4),
                 scales=w_scales[u][:, k].rearrange("p q m -> p (q m)"),
@@ -137,8 +161,10 @@ def tile_locallyconnectednet_pa_t_kernel(tc, h_bytes, h_scale, w2, b2, fc1_w, fc
         def products(u, k, lo, hi):
             for q in range(POS):
                 if (u, q) not in accs:
-                    if u % 2:
-                        accs[u, q] = psum_t.tile([P, NB], F32, name="turned")
+                    if u % 2 and q < 2:
+                        accs[u, q] = psum_h.tile([P, NB], F32, name="turned")
+                    elif u % 2:
+                        accs[u, q] = psum_w.tile([P, NB], F32, name="w_turned")
                     else:
                         accs[u, q] = psum_a.tile([P, NB], F32, name="acc")
                 i, j = q // 2, q % 2
@@ -164,15 +190,14 @@ def tile_locallyconnectednet_pa_t_kernel(tc, h_bytes, h_scale, w2, b2, fc1_w, fc
                 dst = best[u][:] if q < POS - 1 else pooled[:, u, :]
                 nc.vector.scalar_tensor_tensor(out=dst, in0=accs[u, q][:], scalar=b, in1=old[:], op0=ALU.add, op1=ALU.max)
 
-        fc_raw = group_tile([P, T, F], BF16)
+        fc_raw = h_tile([P, T, F], BF16)
         nc.sync.dma_start(out=fc_raw[:], in_=fc1_w.rearrange("(p t) f -> p t f", t=T))
         load_h(0, 0)
         load_h(0, 1)
         nc.sync.dma_start(out=scale[:], in_=h_scale.rearrange("o (p t) a b -> p (o t a b)", t=T))
         load_h(1, 0)
         load_h(1, 1)
-        load_raw(0, 0)
-        fc_grouped = group_tile([P, F, T], BF16)
+        fc_grouped = h_tile([P, F, T], BF16)
         nc.vector.tensor_copy(out=fc_grouped[:], in_=fc_raw[:].rearrange("p t f -> p f t"))
         widen(nc.scalar.copy, 0, 0, 0, 2048)
         widen(nc.vector.tensor_copy, 0, 0, 2048, 4096)
@@ -180,65 +205,63 @@ def tile_locallyconnectednet_pa_t_kernel(tc, h_bytes, h_scale, w2, b2, fc1_w, fc
         widen(nc.vector.tensor_copy, 0, 1, 0, 4096)
         load_h(2, 0)
         load_h(2, 1)
-        load_raw(0, 1)
+        natural = space.tile([P, C * Q], BF16, name="natural", offset=0)
+        nv = w2.rearrange("(m u) c k i j -> u m (c k i j)", u=U)
+        for s in range(4):
+            nc.sync.dma_start(out=natural[:, s * 4608 : (s + 1) * 4608], in_=nv[0][:, s * 4608 : (s + 1) * 4608])
         for half in range(2):
             widen(nc.scalar.copy, 1, half, 0, 4096)
         load_h(3, 0)
         load_h(3, 1)
-        load_raw(1, 0)
-        load_raw(1, 1)
         nc.sync.dma_start(out=fc_bias[:], in_=fc1_b.partition_broadcast(P))
         nc.sync.dma_start(out=bias[:], in_=b2.rearrange("(p u) i j -> p (u i j)", u=U))
+        load_raw(1, 0)
+        load_raw(1, 1)
+        load_raw(2, 0)
 
         h_turn(0)
+        turn_steps = {5: (0,), 6: (1,), 9: (2,), 10: (3,), 11: (4,), 12: (5,), 13: (6,), 14: (7,), 15: (8,)}
+        quantise_steps = {9: (0,), 10: (1,), 12: (2,), 13: (3,), 14: (4,), 15: (5,)}
         for s in range(16):
+            if s in (3, 7):
+                for half in range(2):
+                    widen(nc.scalar.copy, 2 + s // 4, half, 0, 4096)
             if s < 15:
                 h_turn(s + 1)
+            for k in turn_steps.get(s, ()):
+                w_turn(0, k, 0)
+                w_turn(0, k, 2)
             h_scale_step(s)
             if s > 0:
                 h_quantise(s - 1)
-            if s in (3, 7):
-                g = 2 + s // 4
-                for half in range(2):
-                    widen(nc.scalar.copy, g, half, 0, 4096)
-            if s in (4, 7, 8, 9, 10, 11, 12, 13, 14):
-                k = (4, 7, 8, 9, 10, 11, 12, 13, 14).index(s)
-                for half in range(2):
-                    regroup(nc.scalar.copy, 0, k, half)
-            if s in (8, 10, 11, 12, 13, 14, 15):
-                k = (8, 10, 11, 12, 13, 14, 15).index(s)
+            for k in quantise_steps.get(s, ()):
                 w_quantise(0, k)
-                if s == 10:
-                    products(0, 0, 0, 256)
-                if s >= 10:
-                    products(0, k, 0, 256)
-        load_raw(2, 0)
-        load_raw(2, 1)
+                products(0, k, 0, 256)
         h_quantise(15)
+        load_raw(2, 1)
+        load_raw(3, 0)
+        load_raw(3, 1)
 
-        for k in (7, 8):
+        for k in (6, 7, 8):
             w_quantise(0, k)
             products(0, k, 0, 256)
         for k in range(KK):
             products(0, k, 256, 512)
         units = [(u, k) for u in range(1, U) for k in range(KK)]
         for n, (u, k) in enumerate(units):
-            regroup(nc.scalar.copy, u, k, 0)
-            regroup(nc.scalar.copy if n % 5 == 5 - 1 else nc.vector.tensor_copy, u, k, 1)
+            regroup(nc.vector.tensor_copy if n in (0,) else nc.scalar.copy, u, k, 0)
+            regroup(nc.scalar.copy if n in (9, 14, 19, 24) else nc.vector.tensor_copy, u, k, 1)
             if n > 0:
                 w_quantise(*units[n - 1])
                 products(*units[n - 1], 0, NB)
-            if k == KK - 1 and u + 2 < U:
-                load_raw(u + 2, 0)
-                load_raw(u + 2, 1)
-            if k in (2, 4, 5, 6):
-                pool_max(u - 1, (2, 4, 5, 6).index(k))
+            if k in (3, 5, 6, 7):
+                pool_max(u - 1, (3, 5, 6, 7).index(k))
         w_quantise(*units[-1])
         products(*units[-1], 0, NB)
         for q in range(POS):
             pool_max(U - 1, q)
 
-        g_grouped = group_tile([P, NB, U], BF16)
+        g_grouped = h_tile([P, NB, U], BF16)
 
         def dense_group(g):
             cols = slice(g * P, (g + 1) * P)
@@ -267,11 +290,10 @@ def tile_locallyconnectednet_pa_t_kernel(tc, h_bytes, h_scale, w2, b2, fc1_w, fc
 
         def dense_out(g):
             cols = slice(g * P, (g + 1) * P)
-            total = group_tile([P, F], F32)
+            total = w_tile([P, F], F32)
             nc.vector.tensor_tensor(out=total[:], in0=prods[g][:], in1=fc_bias[:], op=ALU.add)
-            res = group_tile([P, F], F32)
-            nc.scalar.activation(res[:], total[:], ACT.Relu)
-            nc.sync.dma_start(out=out[cols, :], in_=res[:])
+            nc.scalar.activation(total[:], total[:], ACT.Relu)
+            nc.sync.dma_start(out=out[cols, :], in_=total[:])
 
         dense_group(0)
         dense_group(1)

@@ -25,10 +25,10 @@ Q = KK * POS
 PIX = 16
 HALF = 64
 
-WIDE_AT = 73728
-BYTES_AT = WIDE_AT + 2 * 16384
-RAW_AT = {(1, 0): 36864, (1, 1): 55296, (2, 0): 145920, (2, 1): 96768, (3, 0): 0, (3, 1): 18432}
-CODES_AT = {0: 122880, 1: 73728, 2: 122880, 3: 73728}
+WIDE_AT = (90112, 73728)
+BYTES_AT = 106496
+RAW_AT = {(0, 0): 0, (0, 1): 18432, (1, 0): 36864, (1, 1): 55296, (2, 0): 104448, (2, 1): 86016, (3, 0): 0, (3, 1): 18432}
+CODES_AT = (122880, 145920, 122880, 145920)
 
 FLOPS = 37 * 2 * 512 * 512 * 512
 
@@ -45,8 +45,8 @@ def tile_locallyconnectednet_pa_t_kernel(tc, h_bytes, h_scale, w2, b2, fc1_w, fc
         psum_w = ctx.enter_context(tc.psum_pool(name="psum_w", bufs=2))
         psum_a = ctx.enter_context(tc.psum_pool(name="psum_a", bufs=4))
 
-        ident = keep.tile([P, P], BF16)
-        make_identity(nc, ident[:])
+        ident_f = keep.tile([P, P], F32)
+        make_identity(nc, ident_f[:])
         ctx.enter_context(tc.manual_schedule())
 
         hb = h_bytes.rearrange("(g n) c a b -> g n (c a b)", n=P)
@@ -60,8 +60,6 @@ def tile_locallyconnectednet_pa_t_kernel(tc, h_bytes, h_scale, w2, b2, fc1_w, fc
         fc_bias = keep.tile([P, F], BF16)
         fc_codes = keep.tile([P, F], U32, align_bytes=64)
         fc_scales = keep.tile([P, F], U8, align_bytes=64)
-        g_codes = keep.tile([P, NB], U32, align_bytes=64)
-        g_scales = keep.tile([P, NB], U8, align_bytes=64)
 
         bytes_tiles = {}
         raws = {}
@@ -98,24 +96,22 @@ def tile_locallyconnectednet_pa_t_kernel(tc, h_bytes, h_scale, w2, b2, fc1_w, fc
 
         def widen(copy, g, half, lo, hi):
             if g not in wides:
-                wides[g] = space.tile([P, C * PIX], BF16, name="wide%d" % (g % 2), offset=WIDE_AT + 16384 * (g % 2))
+                wides[g] = space.tile([P, C * PIX], BF16, name="wide%d" % (g % 2), offset=WIDE_AT[g % 2])
             copy(out=wides[g][:, half * 4096 + lo : half * 4096 + hi], in_=bytes_tiles[g, half][:, lo:hi].bitcast(FP8))
 
-        def h_turn(s):
-            g, x = s // 4, 4 * (s % 4)
-            for y in range(0, 4, 2):
-                turned = psum_h.tile([P, 2, T, P], BF16, name="turned")
-                for z in range(2):
-                    for t in range(T):
-                        nc.tensor.transpose(turned[:, z, t, :], wides[g][:, t * PIX + x + y + z :: T * PIX], ident[:])
-                groups["turned", s, y] = turned
+        def h_turn(s, y):
+            g, word = s // 4, 2 * (s % 4) + y
+            turned = psum_h.tile([P, T, P], F32, name="turned")
+            for t in range(T):
+                nc.tensor.transpose(turned[:, t, :], wides[g][:].bitcast(F32)[:, t * PIX // 2 + word :: T * PIX // 2], ident_f[:])
+            groups["turned", s, y] = turned
 
         def h_scale_step(s):
             grouped = h_tile([P, 4, P, T], BF16)
-            for y in range(0, 4, 2):
+            for y in range(2):
                 nc.vector.tensor_tensor(
-                    out=grouped[:, y : y + 2],
-                    in0=groups["turned", s, y][:].rearrange("p z t n -> p z n t"),
+                    out=grouped[:, 2 * y : 2 * y + 2],
+                    in0=groups["turned", s, y][:].bitcast(BF16).rearrange("p t (n z) -> p z n t", z=2),
                     in1=scale_b,
                     op=ALU.mult,
                 )
@@ -138,15 +134,6 @@ def tile_locallyconnectednet_pa_t_kernel(tc, h_bytes, h_scale, w2, b2, fc1_w, fc
                 in_=raws[u, half][:].rearrange("p m (t q) -> p (m t) q", t=T)[:, :, POS * k : POS * k + POS],
             )
 
-        def w_turn(u, k, y):
-            if (u, k) not in groups:
-                groups[u, k] = unit_tile(u, k)
-            turned = psum_w.tile([P, 2, T, P], BF16, name="w_turned")
-            for z in range(2):
-                for t in range(T):
-                    nc.tensor.transpose(turned[:, z, t, :], natural[:, t * Q + POS * k + y + z :: T * Q], ident[:])
-            nc.scalar.copy(out=groups[u, k][:, y : y + 2], in_=turned[:].rearrange("p z t m -> p z m t"))
-
         def w_quantise(u, k):
             if k == 0:
                 at = CODES_AT[u]
@@ -164,7 +151,7 @@ def tile_locallyconnectednet_pa_t_kernel(tc, h_bytes, h_scale, w2, b2, fc1_w, fc
                     if u % 2 and q < 2:
                         accs[u, q] = psum_h.tile([P, NB], F32, name="turned")
                     elif u % 2:
-                        accs[u, q] = psum_w.tile([P, NB], F32, name="w_turned")
+                        accs[u, q] = psum_w.tile([P, NB], F32, name="planes")
                     else:
                         accs[u, q] = psum_a.tile([P, NB], F32, name="acc")
                 i, j = q // 2, q % 2
@@ -190,77 +177,88 @@ def tile_locallyconnectednet_pa_t_kernel(tc, h_bytes, h_scale, w2, b2, fc1_w, fc
                 dst = best[u][:] if q < POS - 1 else pooled[:, u, :]
                 nc.vector.scalar_tensor_tensor(out=dst, in0=accs[u, q][:], scalar=b, in1=old[:], op0=ALU.add, op1=ALU.max)
 
-        fc_raw = h_tile([P, T, F], BF16)
-        nc.sync.dma_start(out=fc_raw[:], in_=fc1_w.rearrange("(p t) f -> p t f", t=T))
         load_h(0, 0)
         load_h(0, 1)
+        fc_raw = h_tile([P, T, F], BF16)
+        nc.sync.dma_start(out=fc_raw[:], in_=fc1_w.rearrange("(p t) f -> p t f", t=T))
         nc.sync.dma_start(out=scale[:], in_=h_scale.rearrange("o (p t) a b -> p (o t a b)", t=T))
         load_h(1, 0)
         load_h(1, 1)
-        fc_grouped = h_tile([P, F, T], BF16)
-        nc.vector.tensor_copy(out=fc_grouped[:], in_=fc_raw[:].rearrange("p t f -> p f t"))
+        load_raw(0, 0)
         widen(nc.scalar.copy, 0, 0, 0, 2048)
         widen(nc.vector.tensor_copy, 0, 0, 2048, 4096)
-        nc.vector.quantize_mx(out=fc_codes[:].bitcast(FP8X4), scales=fc_scales[:], in_=fc_grouped[:].rearrange("p f t -> p (f t)"))
         widen(nc.vector.tensor_copy, 0, 1, 0, 4096)
+        fc_grouped = h_tile([P, F, T], BF16)
+        nc.vector.tensor_copy(out=fc_grouped[:], in_=fc_raw[:].rearrange("p t f -> p f t"))
+        nc.vector.quantize_mx(out=fc_codes[:].bitcast(FP8X4), scales=fc_scales[:], in_=fc_grouped[:].rearrange("p f t -> p (f t)"))
         load_h(2, 0)
         load_h(2, 1)
-        natural = space.tile([P, C * Q], BF16, name="natural", offset=0)
-        nv = w2.rearrange("(m u) c k i j -> u m (c k i j)", u=U)
-        for s in range(4):
-            nc.sync.dma_start(out=natural[:, s * 4608 : (s + 1) * 4608], in_=nv[0][:, s * 4608 : (s + 1) * 4608])
+        load_raw(0, 1)
         for half in range(2):
             widen(nc.scalar.copy, 1, half, 0, 4096)
         load_h(3, 0)
         load_h(3, 1)
-        nc.sync.dma_start(out=fc_bias[:], in_=fc1_b.partition_broadcast(P))
-        nc.sync.dma_start(out=bias[:], in_=b2.rearrange("(p u) i j -> p (u i j)", u=U))
         load_raw(1, 0)
         load_raw(1, 1)
-        load_raw(2, 0)
+        nc.sync.dma_start(out=fc_bias[:], in_=fc1_b.partition_broadcast(P))
+        nc.sync.dma_start(out=bias[:], in_=b2.rearrange("(p u) i j -> p (u i j)", u=U))
 
-        h_turn(0)
-        turn_steps = {5: (0,), 6: (1,), 9: (2,), 10: (3,), 11: (4,), 12: (5,), 13: (6,), 14: (7,), 15: (8,)}
-        quantise_steps = {9: (0,), 10: (1,), 12: (2,), 13: (3,), 14: (4,), 15: (5,)}
+        units = [(u, k) for u in range(1, U) for k in range(KK)]
+        h_turn(0, 0)
+        h_turn(0, 1)
+        on_tensor = {3: ((0, 0), (1, 0), (2, 0)), 7: ((0, 1), (1, 1), (2, 1)), 11: ((3, 0), (3, 1)), 12: ((4, 0), (4, 1), (5, 0), (5, 1)), 13: ((6, 0), (6, 1), (7, 0), (7, 1)), 14: ((8, 0), (8, 1))}
+        quantise = {10: (0,), 11: (1, 2), 12: (3,), 13: (4,), 14: (5,), 15: (6,)}
+        ahead = {}
         for s in range(16):
             if s in (3, 7):
+                if s == 3:
+                    for k, half in on_tensor[s]:
+                        regroup(nc.scalar.copy, 0, k, half)
                 for half in range(2):
                     widen(nc.scalar.copy, 2 + s // 4, half, 0, 4096)
-            if s < 15:
-                h_turn(s + 1)
-            for k in turn_steps.get(s, ()):
-                w_turn(0, k, 0)
-                w_turn(0, k, 2)
+            jobs = list(on_tensor.get(s, ())) if s != 3 else []
+            for n in range(2):
+                if s < 15:
+                    h_turn(s + 1, n)
+                for k, half in jobs[n::2]:
+                    regroup(nc.scalar.copy, 0, k, half)
+            for n in ahead.get(s, ()):
+                for half in range(2):
+                    regroup(nc.scalar.copy, *units[n], half)
             h_scale_step(s)
             if s > 0:
                 h_quantise(s - 1)
-            for k in quantise_steps.get(s, ()):
+            for k in quantise.get(s, ()):
                 w_quantise(0, k)
                 products(0, k, 0, 256)
         h_quantise(15)
+        load_raw(2, 0)
         load_raw(2, 1)
         load_raw(3, 0)
         load_raw(3, 1)
 
-        for k in (6, 7, 8):
+        for k in (7, 8):
             w_quantise(0, k)
             products(0, k, 0, 256)
         for k in range(KK):
             products(0, k, 256, 512)
-        units = [(u, k) for u in range(1, U) for k in range(KK)]
+        done = [n for s in ahead for n in ahead[s]]
         for n, (u, k) in enumerate(units):
-            regroup(nc.vector.tensor_copy if n in (0,) else nc.scalar.copy, u, k, 0)
-            regroup(nc.scalar.copy if n in (9, 14, 19, 24) else nc.vector.tensor_copy, u, k, 1)
+            if n not in done:
+                regroup(nc.vector.tensor_copy if n in () else nc.scalar.copy, u, k, 0)
+                regroup(nc.scalar.copy if n in (8, 12, 20) else nc.vector.tensor_copy, u, k, 1)
             if n > 0:
                 w_quantise(*units[n - 1])
                 products(*units[n - 1], 0, NB)
-            if k in (3, 5, 6, 7):
-                pool_max(u - 1, (3, 5, 6, 7).index(k))
+            if k in (4, 6, 7, 8):
+                pool_max(u - 1, (4, 6, 7, 8).index(k))
         w_quantise(*units[-1])
         products(*units[-1], 0, NB)
         for q in range(POS):
             pool_max(U - 1, q)
 
+        g_codes = space.tile([P, NB], U32, align_bytes=64, name="g_codes", offset=RAW_AT[1, 0])
+        g_scales = space.tile([P, NB], U8, align_bytes=64, name="g_scales", offset=RAW_AT[1, 0] + 2048)
         g_grouped = h_tile([P, NB, U], BF16)
 
         def dense_group(g):
@@ -290,7 +288,7 @@ def tile_locallyconnectednet_pa_t_kernel(tc, h_bytes, h_scale, w2, b2, fc1_w, fc
 
         def dense_out(g):
             cols = slice(g * P, (g + 1) * P)
-            total = w_tile([P, F], F32)
+            total = (h_tile if g == 3 else w_tile)([P, F], F32)
             nc.vector.tensor_tensor(out=total[:], in0=prods[g][:], in1=fc_bias[:], op=ALU.add)
             nc.scalar.activation(total[:], total[:], ACT.Relu)
             nc.sync.dma_start(out=out[cols, :], in_=total[:])

@@ -30,6 +30,14 @@ BYTES_AT = 106496
 RAW_AT = {(0, 0): 0, (0, 1): 18432, (1, 0): 36864, (1, 1): 55296, (2, 0): 104448, (2, 1): 86016, (3, 0): 0, (3, 1): 18432}
 CODES_AT = (122880, 145920, 122880, 145920)
 
+
+def unit_list(u):
+    if u < U - 1:
+        return [[(k, q) for q in range(POS)] for k in range(KK)]
+    pairs = [[[(k, 2 * i), (k, 2 * i + 1), (k + 1, 2 * i), (k + 1, 2 * i + 1)] for k in range(0, KK - 1, 2)] for i in range(2)]
+    return pairs[0] + [[(KK - 1, q) for q in range(POS)]] + pairs[1]
+
+
 FLOPS = 37 * 2 * 512 * 512 * 512
 
 
@@ -40,9 +48,9 @@ def tile_locallyconnectednet_pa_t_kernel(tc, h_bytes, h_scale, w2, b2, fc1_w, fc
         space = ctx.enter_context(tc.tile_pool(name="space", bufs=1))
         h_pool = ctx.enter_context(tc.tile_pool(name="h_pool", bufs=2))
         w_pool = ctx.enter_context(tc.tile_pool(name="w_pool", bufs=3))
+        token_pool = ctx.enter_context(tc.tile_pool(name="token_pool", bufs=1))
         max_pool = ctx.enter_context(tc.tile_pool(name="max_pool", bufs=2))
-        psum_h = ctx.enter_context(tc.psum_pool(name="psum_h", bufs=2))
-        psum_w = ctx.enter_context(tc.psum_pool(name="psum_w", bufs=2))
+        psum_h = ctx.enter_context(tc.psum_pool(name="psum_h", bufs=4))
         psum_a = ctx.enter_context(tc.psum_pool(name="psum_a", bufs=4))
 
         ident_f = keep.tile([P, P], F32)
@@ -68,6 +76,7 @@ def tile_locallyconnectednet_pa_t_kernel(tc, h_bytes, h_scale, w2, b2, fc1_w, fc
         w_codes = {}
         w_scales = {}
         accs = {}
+        tokens = [None]
         best = {}
 
         def h_tile(shape, dtype):
@@ -77,14 +86,21 @@ def tile_locallyconnectednet_pa_t_kernel(tc, h_bytes, h_scale, w2, b2, fc1_w, fc
             return w_pool.tile(shape, dtype, align_bytes=64, name="w_grouped")
 
         def unit_tile(u, k):
-            if u > 0 and ((u - 1) * KK + k) % 5 > 2:
+            n = (u - 1) * KK + k
+            if u == 0 and k < 5:
+                return space.tile([P, POS, P, T], BF16, align_bytes=64, name="early%d" % k, offset=CODES_AT[1] + 4096 * k)
+            if u > 0 and n % 8 in (3, 4, 5):
+                return space.tile([P, POS, P, T], BF16, align_bytes=64, name="late%d" % (n % 8), offset=73728 + 4096 * (n % 8 - 3))
+            if u > 0 and n % 8 in (6, 7):
                 return h_tile([P, POS, P, T], BF16)
             return w_tile([P, POS, P, T], BF16)
 
         def load_h(g, half):
             n = (2 * g + half) % 4
             raw_bytes = space.tile([P, C * PIX // 2], U8, name="raw_bytes%d" % n, offset=BYTES_AT + 4096 * n)
-            nc.sync.dma_start(out=raw_bytes[:], in_=hb[g][:, half * 4096 : half * 4096 + 4096])
+            step = 2048 if g == 0 else 4096
+            for lo in range(0, 4096, step):
+                nc.sync.dma_start(out=raw_bytes[:, lo : lo + step], in_=hb[g][:, half * 4096 + lo : half * 4096 + lo + step])
             bytes_tiles[g, half] = raw_bytes
 
         def load_raw(u, half):
@@ -129,13 +145,33 @@ def tile_locallyconnectednet_pa_t_kernel(tc, h_bytes, h_scale, w2, b2, fc1_w, fc
         def regroup(copy, u, k, half):
             if (u, k) not in groups:
                 groups[u, k] = unit_tile(u, k)
-            copy(
-                out=groups[u, k][:, :, half * HALF : (half + 1) * HALF, :].rearrange("p q m t -> p (m t) q"),
-                in_=raws[u, half][:].rearrange("p m (t q) -> p (m t) q", t=T)[:, :, POS * k : POS * k + POS],
+            (k0, q0), (k3, q3) = unit_list(u)[k][0], unit_list(u)[k][3]
+            dst = groups[u, k][:, :, half * HALF : (half + 1) * HALF, :]
+            if k0 == k3:
+                copy(
+                    out=dst.rearrange("p q m t -> p (m t) q"),
+                    in_=raws[u, half][:].rearrange("p m (t q) -> p (m t) q", t=T)[:, :, POS * k0 : POS * k0 + POS],
+                )
+            else:
+                copy(
+                    out=dst.rearrange("p (k j) m t -> p (m t) k j", j=2),
+                    in_=raws[u, half][:].rearrange("p m (t k i j) -> p (m t) k i j", t=T, i=2, j=2)[:, :, k0 : k0 + 2, q0 // 2, :],
+                )
+
+        def regroup_on_gpsimd(u, k, half):
+            if (u, k) not in groups:
+                groups[u, k] = unit_tile(u, k)
+            nc.gpsimd.tensor_scalar(
+                out=groups[u, k][:, :, half * HALF : (half + 1) * HALF, :].rearrange("p q m t -> p m q t"),
+                in0=raws[u, half][:].rearrange("p m (t q) -> p m q t", t=T)[:, :, POS * k : POS * k + POS, :],
+                scalar1=tokens[0][:],
+                scalar2=0.0,
+                op0=ALU.mult,
+                op1=ALU.add,
             )
 
         def w_quantise(u, k):
-            if k == 0:
+            if u not in w_codes:
                 at = CODES_AT[u]
                 w_codes[u] = space.tile([P, KK, POS, P], U32, align_bytes=64, name="w_codes%d" % at, offset=at)
                 w_scales[u] = space.tile([P, KK, POS, P], U8, align_bytes=64, name="w_scales%d" % at, offset=at + 18432)
@@ -145,25 +181,24 @@ def tile_locallyconnectednet_pa_t_kernel(tc, h_bytes, h_scale, w2, b2, fc1_w, fc
                 in_=groups[u, k][:].rearrange("p q m t -> p (q m t)"),
             )
 
-        def products(u, k, lo, hi):
-            for q in range(POS):
+        def products(u, n, lo, hi, runs=tuple(range(KK))):
+            for c, (k, q) in enumerate(unit_list(u)[n]):
+                order = [kk for r in runs for kk, qq in unit_list(u)[r] if qq == q]
                 if (u, q) not in accs:
-                    if u % 2 and q < 2:
+                    if u % 2:
                         accs[u, q] = psum_h.tile([P, NB], F32, name="turned")
-                    elif u % 2:
-                        accs[u, q] = psum_w.tile([P, NB], F32, name="planes")
                     else:
                         accs[u, q] = psum_a.tile([P, NB], F32, name="acc")
                 i, j = q // 2, q % 2
                 pix = (k // 3 + i) * 4 + k % 3 + j
                 nc.tensor.matmul_mx(
                     out=accs[u, q][:, lo:hi],
-                    lhsT=w_codes[u][:, k, q, :].bitcast(FP8X4),
-                    lhsT_scale=w_scales[u][:, k, q, :],
+                    lhsT=w_codes[u][:, n, c, :].bitcast(FP8X4),
+                    lhsT_scale=w_scales[u][:, n, c, :],
                     rhs=h_codes[:, pix, lo:hi].bitcast(FP8X4),
                     rhs_scale=h_scales[:, pix, lo:hi],
-                    start=(k == 0),
-                    stop=(k == KK - 1),
+                    start=(k == order[0]),
+                    stop=(k == order[-1]),
                 )
 
         def pool_max(u, q):
@@ -185,8 +220,8 @@ def tile_locallyconnectednet_pa_t_kernel(tc, h_bytes, h_scale, w2, b2, fc1_w, fc
         load_h(1, 0)
         load_h(1, 1)
         load_raw(0, 0)
-        widen(nc.scalar.copy, 0, 0, 0, 2048)
-        widen(nc.vector.tensor_copy, 0, 0, 2048, 4096)
+        widen(nc.vector.tensor_copy, 0, 0, 0, 2048)
+        widen(nc.scalar.copy, 0, 0, 2048, 4096)
         widen(nc.vector.tensor_copy, 0, 1, 0, 4096)
         fc_grouped = h_tile([P, F, T], BF16)
         nc.vector.tensor_copy(out=fc_grouped[:], in_=fc_raw[:].rearrange("p t f -> p f t"))
@@ -206,64 +241,83 @@ def tile_locallyconnectednet_pa_t_kernel(tc, h_bytes, h_scale, w2, b2, fc1_w, fc
         units = [(u, k) for u in range(1, U) for k in range(KK)]
         h_turn(0, 0)
         h_turn(0, 1)
-        on_tensor = {3: ((0, 0), (1, 0), (2, 0)), 7: ((0, 1), (1, 1), (2, 1)), 11: ((3, 0), (3, 1)), 12: ((4, 0), (4, 1), (5, 0), (5, 1)), 13: ((6, 0), (6, 1), (7, 0), (7, 1)), 14: ((8, 0), (8, 1))}
-        quantise = {10: (0,), 11: (1, 2), 12: (3,), 13: (4,), 14: (5,), 15: (6,)}
-        ahead = {}
+        on_scalar = {
+            3: (2,),
+            7: (3,),
+            11: ((0, 8, 0), (0, 8, 1)),
+            12: ((0, 7, 0), (0, 7, 1)),
+            13: ((0, 6, 0), (0, 6, 1), (0, 5, 0), (0, 5, 1)),
+            14: ((1, 0, 0), (1, 1, 0), (1, 0, 1), (1, 1, 1)),
+            15: ((1, 2, 0), (1, 2, 1)),
+        }
+        quantise = {9: ((0, 0),), 10: ((0, 1),), 11: ((0, 2),), 12: ((0, 3), (0, 8)), 13: ((0, 4), (0, 7)), 14: ((0, 6),), 15: ((0, 5), (1, 0))}
+        on_gpsimd = {3: (0, 0), 4: (1, 0), 5: (2, 0), 6: (3, 0), 7: (4, 0), 8: (0, 1), 9: (1, 1), 10: (2, 1), 11: (3, 1), 12: (4, 1)}
+        first = (0, 1, 2, 3, 8, 4, 7, 6, 5)
         for s in range(16):
-            if s in (3, 7):
-                if s == 3:
-                    for k, half in on_tensor[s]:
-                        regroup(nc.scalar.copy, 0, k, half)
-                for half in range(2):
-                    widen(nc.scalar.copy, 2 + s // 4, half, 0, 4096)
-            jobs = list(on_tensor.get(s, ())) if s != 3 else []
+            for job in on_scalar.get(s, ()):
+                if job in (2, 3):
+                    for half in range(2):
+                        widen(nc.scalar.copy, job, half, 0, 4096)
+                else:
+                    regroup(nc.scalar.copy, *job)
             for n in range(2):
                 if s < 15:
                     h_turn(s + 1, n)
-                for k, half in jobs[n::2]:
-                    regroup(nc.scalar.copy, 0, k, half)
-            for n in ahead.get(s, ()):
-                for half in range(2):
-                    regroup(nc.scalar.copy, *units[n], half)
+            if s in on_gpsimd:
+                tokens[0] = token_pool.tile([P, 1], F32, name="token")
+                nc.vector.memset(tokens[0][:], 1.0)
+                regroup_on_gpsimd(0, *on_gpsimd[s])
             h_scale_step(s)
             if s > 0:
                 h_quantise(s - 1)
-            for k in quantise.get(s, ()):
-                w_quantise(0, k)
-                products(0, k, 0, 256)
+            for u, k in quantise.get(s, ()):
+                w_quantise(u, k)
+                if u == 0:
+                    products(0, k, 0, 256, first)
         h_quantise(15)
         load_raw(2, 0)
         load_raw(2, 1)
         load_raw(3, 0)
         load_raw(3, 1)
 
-        for k in (7, 8):
-            w_quantise(0, k)
-            products(0, k, 0, 256)
-        for k in range(KK):
-            products(0, k, 256, 512)
-        done = [n for s in ahead for n in ahead[s]]
+        for k in first:
+            products(0, k, 256, 512, first)
+        quantised = [(u, k) for s in quantise for u, k in quantise[s] if u > 0]
+        for u, k in quantised:
+            products(u, k, 0, NB)
+        scalar_did = [job for s in on_scalar for job in on_scalar[s] if job not in (2, 3)]
+        max_at = {7: (0, 0), 8: (0, 1), 9: (0, 2), 10: (0, 3), 14: (1, 0), 15: (1, 1), 16: (1, 2), 17: (1, 3), 21: (2, 0), 22: (2, 1), 23: (2, 2), 24: (2, 3), 25: (3, 0)}
         for n, (u, k) in enumerate(units):
-            if n not in done:
-                regroup(nc.vector.tensor_copy if n in () else nc.scalar.copy, u, k, 0)
-                regroup(nc.scalar.copy if n in (8, 12, 20) else nc.vector.tensor_copy, u, k, 1)
-            if n > 0:
+            for half in range(2):
+                if (u, k, half) not in scalar_did:
+                    on_vector = (n in ()) if half == 0 else (n not in ())
+                    regroup(nc.vector.tensor_copy if on_vector else nc.scalar.copy, u, k, half)
+            if n > 0 and units[n - 1] not in quantised:
                 w_quantise(*units[n - 1])
                 products(*units[n - 1], 0, NB)
-            if k in (4, 6, 7, 8):
-                pool_max(u - 1, (4, 6, 7, 8).index(k))
+            if n in max_at:
+                pool_max(*max_at[n])
         w_quantise(*units[-1])
         products(*units[-1], 0, NB)
-        for q in range(POS):
-            pool_max(U - 1, q)
+        pool_max(U - 1, 1)
+        pool_max(U - 1, 2)
+        for lo in (0, 256):
+            nc.vector.scalar_tensor_tensor(
+                out=pooled[:, U - 1, lo : lo + 256],
+                in0=accs[U - 1, 3][:, lo : lo + 256],
+                scalar=bias[:, POS * U - 1 : POS * U],
+                in1=best[U - 1][:, lo : lo + 256],
+                op0=ALU.add,
+                op1=ALU.max,
+            )
 
         g_codes = space.tile([P, NB], U32, align_bytes=64, name="g_codes", offset=RAW_AT[1, 0])
         g_scales = space.tile([P, NB], U8, align_bytes=64, name="g_scales", offset=RAW_AT[1, 0] + 2048)
         g_grouped = h_tile([P, NB, U], BF16)
 
-        def dense_group(g):
+        def dense_group(copy, g):
             cols = slice(g * P, (g + 1) * P)
-            nc.vector.tensor_copy(out=g_grouped[:, cols, :], in_=pooled[:, :, cols].rearrange("p u n -> p n u"))
+            copy(out=g_grouped[:, cols, :], in_=pooled[:, :, cols].rearrange("p u n -> p n u"))
 
         def dense_quantise(g):
             cols = slice(g * P, (g + 1) * P)
@@ -293,17 +347,14 @@ def tile_locallyconnectednet_pa_t_kernel(tc, h_bytes, h_scale, w2, b2, fc1_w, fc
             nc.scalar.activation(total[:], total[:], ACT.Relu)
             nc.sync.dma_start(out=out[cols, :], in_=total[:])
 
-        dense_group(0)
-        dense_group(1)
+        dense_group(nc.vector.tensor_copy, 0)
+        dense_group(nc.scalar.copy, 1)
         dense_quantise(0)
         dense_product(0)
-        dense_group(2)
-        dense_quantise(1)
-        dense_product(1)
-        dense_group(3)
-        dense_quantise(2)
-        dense_product(2)
-        dense_quantise(3)
-        dense_product(3)
+        dense_group(nc.vector.tensor_copy, 2)
+        dense_group(nc.scalar.copy, 3)
+        for g in range(1, G):
+            dense_quantise(g)
+            dense_product(g)
         for g in range(G):
             dense_out(g)

@@ -89,6 +89,8 @@ def tile_locallyconnectednet_pa_t_kernel(tc, h_bytes, h_scale, w2, b2, fc1_w, fc
             n = (u - 1) * KK + k
             if u == 0 and k < 5:
                 return space.tile([P, POS, P, T], BF16, align_bytes=64, name="early%d" % k, offset=CODES_AT[1] + 4096 * k)
+            if u == U - 1:
+                return space.tile([P, POS, P, T], BF16, align_bytes=64, name="last%d" % k, offset=RAW_AT[1, 0] + 4096 * k)
             if u > 0 and n % 8 in (3, 4, 5):
                 return space.tile([P, POS, P, T], BF16, align_bytes=64, name="late%d" % (n % 8), offset=73728 + 4096 * (n % 8 - 3))
             if u > 0 and n % 8 in (6, 7):
@@ -142,20 +144,20 @@ def tile_locallyconnectednet_pa_t_kernel(tc, h_bytes, h_scale, w2, b2, fc1_w, fc
                     in_=groups["h", s][:, y].rearrange("p n t -> p (n t)"),
                 )
 
-        def regroup(copy, u, k, half):
+        def regroup(copy, u, k, half, lo=0, hi=HALF):
             if (u, k) not in groups:
                 groups[u, k] = unit_tile(u, k)
             (k0, q0), (k3, q3) = unit_list(u)[k][0], unit_list(u)[k][3]
-            dst = groups[u, k][:, :, half * HALF : (half + 1) * HALF, :]
+            dst = groups[u, k][:, :, half * HALF + lo : half * HALF + hi, :]
             if k0 == k3:
                 copy(
                     out=dst.rearrange("p q m t -> p (m t) q"),
-                    in_=raws[u, half][:].rearrange("p m (t q) -> p (m t) q", t=T)[:, :, POS * k0 : POS * k0 + POS],
+                    in_=raws[u, half][:, lo:hi].rearrange("p m (t q) -> p (m t) q", t=T)[:, :, POS * k0 : POS * k0 + POS],
                 )
             else:
                 copy(
                     out=dst.rearrange("p (k j) m t -> p (m t) k j", j=2),
-                    in_=raws[u, half][:].rearrange("p m (t k i j) -> p (m t) k i j", t=T, i=2, j=2)[:, :, k0 : k0 + 2, q0 // 2, :],
+                    in_=raws[u, half][:, lo:hi].rearrange("p m (t k i j) -> p (m t) k i j", t=T, i=2, j=2)[:, :, k0 : k0 + 2, q0 // 2, :],
                 )
 
         def regroup_on_gpsimd(u, k, half):
@@ -181,8 +183,10 @@ def tile_locallyconnectednet_pa_t_kernel(tc, h_bytes, h_scale, w2, b2, fc1_w, fc
                 in_=groups[u, k][:].rearrange("p q m t -> p (q m t)"),
             )
 
-        def products(u, n, lo, hi, runs=tuple(range(KK))):
+        def products(u, n, lo, hi, runs=tuple(range(KK)), wanted=(0, 1, 2, 3)):
             for c, (k, q) in enumerate(unit_list(u)[n]):
+                if q not in wanted:
+                    continue
                 order = [kk for r in runs for kk, qq in unit_list(u)[r] if qq == q]
                 if (u, q) not in accs:
                     if u % 2:
@@ -214,8 +218,6 @@ def tile_locallyconnectednet_pa_t_kernel(tc, h_bytes, h_scale, w2, b2, fc1_w, fc
 
         load_h(0, 0)
         load_h(0, 1)
-        fc_raw = h_tile([P, T, F], BF16)
-        nc.sync.dma_start(out=fc_raw[:], in_=fc1_w.rearrange("(p t) f -> p t f", t=T))
         nc.sync.dma_start(out=scale[:], in_=h_scale.rearrange("o (p t) a b -> p (o t a b)", t=T))
         load_h(1, 0)
         load_h(1, 1)
@@ -223,9 +225,6 @@ def tile_locallyconnectednet_pa_t_kernel(tc, h_bytes, h_scale, w2, b2, fc1_w, fc
         widen(nc.vector.tensor_copy, 0, 0, 0, 2048)
         widen(nc.scalar.copy, 0, 0, 2048, 4096)
         widen(nc.vector.tensor_copy, 0, 1, 0, 4096)
-        fc_grouped = h_tile([P, F, T], BF16)
-        nc.vector.tensor_copy(out=fc_grouped[:], in_=fc_raw[:].rearrange("p t f -> p f t"))
-        nc.vector.quantize_mx(out=fc_codes[:].bitcast(FP8X4), scales=fc_scales[:], in_=fc_grouped[:].rearrange("p f t -> p (f t)"))
         load_h(2, 0)
         load_h(2, 1)
         load_raw(0, 1)
@@ -235,7 +234,6 @@ def tile_locallyconnectednet_pa_t_kernel(tc, h_bytes, h_scale, w2, b2, fc1_w, fc
         load_h(3, 1)
         load_raw(1, 0)
         load_raw(1, 1)
-        nc.sync.dma_start(out=fc_bias[:], in_=fc1_b.partition_broadcast(P))
         nc.sync.dma_start(out=bias[:], in_=b2.rearrange("(p u) i j -> p (u i j)", u=U))
 
         units = [(u, k) for u in range(1, U) for k in range(KK)]
@@ -286,31 +284,57 @@ def tile_locallyconnectednet_pa_t_kernel(tc, h_bytes, h_scale, w2, b2, fc1_w, fc
         for u, k in quantised:
             products(u, k, 0, NB)
         scalar_did = [job for s in on_scalar for job in on_scalar[s] if job not in (2, 3)]
-        max_at = {7: (0, 0), 8: (0, 1), 9: (0, 2), 10: (0, 3), 14: (1, 0), 15: (1, 1), 16: (1, 2), 17: (1, 3), 21: (2, 0), 22: (2, 1), 23: (2, 2), 24: (2, 3), 25: (3, 0)}
-        for n, (u, k) in enumerate(units):
+        max_at = {7: (0, 0), 8: (0, 1), 9: (0, 2), 10: (0, 3), 14: (1, 0), 15: (1, 1), 16: (1, 2), 17: (1, 3)}
+        for n, (u, k) in enumerate(units[: 2 * KK]):
             for half in range(2):
                 if (u, k, half) not in scalar_did:
-                    on_vector = (n in ()) if half == 0 else (n not in ())
+                    on_vector = half == 1 and n not in ()
                     regroup(nc.vector.tensor_copy if on_vector else nc.scalar.copy, u, k, half)
             if n > 0 and units[n - 1] not in quantised:
                 w_quantise(*units[n - 1])
                 products(*units[n - 1], 0, NB)
             if n in max_at:
                 pool_max(*max_at[n])
-        w_quantise(*units[-1])
-        products(*units[-1], 0, NB)
-        pool_max(U - 1, 1)
-        pool_max(U - 1, 2)
-        for lo in (0, 256):
-            nc.vector.scalar_tensor_tensor(
-                out=pooled[:, U - 1, lo : lo + 256],
-                in0=accs[U - 1, 3][:, lo : lo + 256],
-                scalar=bias[:, POS * U - 1 : POS * U],
-                in1=best[U - 1][:, lo : lo + 256],
-                op0=ALU.add,
-                op1=ALU.max,
-            )
 
+        fc_raw = w_tile([P, T, F], BF16)
+        nc.sync.dma_start(out=fc_raw[:], in_=fc1_w.rearrange("(p t) f -> p t f", t=T))
+        nc.sync.dma_start(out=fc_bias[:], in_=fc1_b.partition_broadcast(P))
+        last = U - 1
+        for k in (0, 1):
+            regroup(nc.scalar.copy, last, k, 0)
+        w_quantise(*units[2 * KK - 1])
+        products(*units[2 * KK - 1], 0, NB)
+        pool_max(last - 1, 0)
+        for k in (2, 3):
+            regroup(nc.scalar.copy, last, k, 0)
+        for k in (4, 5, 6, 7, 8):
+            regroup(nc.vector.tensor_copy, last, k, 0)
+        for q in range(1, POS):
+            pool_max(last - 1, q)
+        for k in range(KK):
+            regroup(nc.vector.tensor_copy if k in (0, 1) else nc.scalar.copy, last, k, 1, 0, 32)
+        warm = psum_a.tile([P, 3 * P], F32, name="acc")
+        for k in (2, 3, 4, 0, 1):
+            nc.tensor.matmul(
+                warm[:],
+                lhsT=groups[last, k][:, 0, :32].rearrange("p m t -> p (m t)"),
+                rhs=groups[last, k][:, 1, : HALF + 32].rearrange("p m t -> p (m t)"),
+                start=True,
+                stop=True,
+            )
+        for k in range(KK):
+            regroup(nc.vector.tensor_copy if k in (0, 1) else nc.scalar.copy, last, k, 1, 32, 64)
+            w_quantise(last, k)
+            products(last, k, 0, NB, wanted=(0, 1, 2))
+        for lo in (0, 256):
+            for k in range(KK):
+                products(last, k, lo, lo + 256, wanted=(3,))
+        pool_max(last, 0)
+        fc_grouped = w_tile([P, F, T], BF16)
+        nc.scalar.copy(out=fc_grouped[:], in_=fc_raw[:].rearrange("p t f -> p f t"))
+        pool_max(last, 1)
+        pool_max(last, 2)
+        nc.vector.quantize_mx(out=fc_codes[:].bitcast(FP8X4), scales=fc_scales[:], in_=fc_grouped[:].rearrange("p f t -> p (f t)"))
         g_codes = space.tile([P, NB], U32, align_bytes=64, name="g_codes", offset=RAW_AT[1, 0])
         g_scales = space.tile([P, NB], U8, align_bytes=64, name="g_scales", offset=RAW_AT[1, 0] + 2048)
         g_grouped = h_tile([P, NB, U], BF16)
@@ -347,14 +371,31 @@ def tile_locallyconnectednet_pa_t_kernel(tc, h_bytes, h_scale, w2, b2, fc1_w, fc
             nc.scalar.activation(total[:], total[:], ACT.Relu)
             nc.sync.dma_start(out=out[cols, :], in_=total[:])
 
-        dense_group(nc.vector.tensor_copy, 0)
+        def last_max(lo):
+            nc.vector.scalar_tensor_tensor(
+                out=pooled[:, U - 1, lo : lo + 256],
+                in0=accs[U - 1, 3][:, lo : lo + 256],
+                scalar=bias[:, POS * U - 1 : POS * U],
+                in1=best[U - 1][:, lo : lo + 256],
+                op0=ALU.add,
+                op1=ALU.max,
+            )
+
+        last_max(0)
         dense_group(nc.scalar.copy, 1)
+        dense_group(nc.vector.tensor_copy, 0)
         dense_quantise(0)
         dense_product(0)
-        dense_group(nc.vector.tensor_copy, 2)
+        dense_quantise(1)
+        dense_product(1)
+        last_max(256)
         dense_group(nc.scalar.copy, 3)
-        for g in range(1, G):
-            dense_quantise(g)
-            dense_product(g)
-        for g in range(G):
-            dense_out(g)
+        dense_group(nc.vector.tensor_copy, 2)
+        dense_out(0)
+        dense_quantise(2)
+        dense_product(2)
+        dense_quantise(3)
+        dense_product(3)
+        dense_out(1)
+        dense_out(2)
+        dense_out(3)

from contextlib import ExitStack

import concourse.mybir as mybir
from concourse.masks import make_identity

F32 = mybir.dt.float32
BF16 = mybir.dt.bfloat16
U32 = mybir.dt.uint32
U8 = mybir.dt.uint8
FP8 = mybir.dt.float8_e4m3fn
FP8X4 = mybir.dt.float8_e4m3fn_x4
ALU = mybir.AluOpType
ACT = mybir.ActivationFunctionType

P = 128
NB = 512
C = 512
F = 512
T = 4
G = NB // P
U = 4
KK = 9
POS = 4
Q = KK * POS
PIX = 16
HALF = 64

WIDE_AT = (90112, 73728)
BYTES_AT = 106496
RAW_AT = {(0, 0): 0, (0, 1): 18432, (1, 0): 36864, (1, 1): 55296, (2, 0): 104448, (2, 1): 86016, (3, 0): 0, (3, 1): 18432}
CODES_AT = (122880, 145920, 122880, 145920)


def unit_list(u):
    if u < U - 1:
        return [[(k, q) for q in range(POS)] for k in range(KK)]
    pairs = [[[(k, 2 * i), (k, 2 * i + 1), (k + 1, 2 * i), (k + 1, 2 * i + 1)] for k in range(0, KK - 1, 2)] for i in range(2)]
    return pairs[0] + [[(KK - 1, q) for q in range(POS)]] + pairs[1]


FLOPS = 37 * 2 * 512 * 512 * 512


def tile_locallyconnectednet_pa_t_kernel(tc, h_bytes, h_scale, w2, b2, fc1_w, fc1_b, out):
    nc = tc.nc
    with ExitStack() as ctx:
        keep = ctx.enter_context(tc.tile_pool(name="keep", bufs=1))
        space = ctx.enter_context(tc.tile_pool(name="space", bufs=1))
        h_pool = ctx.enter_context(tc.tile_pool(name="h_pool", bufs=2))
        w_pool = ctx.enter_context(tc.tile_pool(name="w_pool", bufs=3))
        token_pool = ctx.enter_context(tc.tile_pool(name="token_pool", bufs=1))
        max_pool = ctx.enter_context(tc.tile_pool(name="max_pool", bufs=2))
        psum_h = ctx.enter_context(tc.psum_pool(name="psum_h", bufs=4))
        psum_a = ctx.enter_context(tc.psum_pool(name="psum_a", bufs=4))

        ident_f = keep.tile([P, P], F32)
        make_identity(nc, ident_f[:])
        ctx.enter_context(tc.manual_schedule())

        hb = h_bytes.rearrange("(g n) c a b -> g n (c a b)", n=P)
        wv = w2.rearrange("(m u) (p t) k i j -> u p m (t k i j)", u=U, t=T)
        h_codes = keep.tile([P, PIX, NB], U32, align_bytes=64)
        h_scales = keep.tile([P, PIX, NB], U8, align_bytes=64)
        pooled = keep.tile([P, U, NB], BF16)
        scale = keep.tile([P, T], F32)
        scale_b = scale[:].unsqueeze(1).unsqueeze(1).to_broadcast([P, 2, P, T])
        bias = keep.tile([P, U * POS], BF16)
        fc_bias = keep.tile([P, F], BF16)
        fc_codes = keep.tile([P, F], U32, align_bytes=64)
        fc_scales = keep.tile([P, F], U8, align_bytes=64)

        bytes_tiles = {}
        raws = {}
        wides = {}
        groups = {}
        w_codes = {}
        w_scales = {}
        accs = {}
        tokens = [None]
        best = {}

        def h_tile(shape, dtype):
            return h_pool.tile(shape, dtype, align_bytes=64, name="h_grouped")

        def w_tile(shape, dtype):
            return w_pool.tile(shape, dtype, align_bytes=64, name="w_grouped")

        def unit_tile(u, k):
            n = (u - 1) * KK + k
            if u == 0 and k < 5:
                return space.tile([P, POS, P, T], BF16, align_bytes=64, name="early%d" % k, offset=CODES_AT[1] + 4096 * k)
            if u == U - 1:
                return space.tile([P, POS, P, T], BF16, align_bytes=64, name="last%d" % k, offset=RAW_AT[1, 0] + 4096 * k)
            if u > 0 and n % 8 in (3, 4, 5):
                return space.tile([P, POS, P, T], BF16, align_bytes=64, name="late%d" % (n % 8), offset=73728 + 4096 * (n % 8 - 3))
            if u > 0 and n % 8 in (6, 7):
                return h_tile([P, POS, P, T], BF16)
            return w_tile([P, POS, P, T], BF16)

        def load_h(g, half):
            n = (2 * g + half) % 4
            raw_bytes = space.tile([P, C * PIX // 2], U8, name="raw_bytes%d" % n, offset=BYTES_AT + 4096 * n)
            step = 2048 if g == 0 else 4096
            for lo in range(0, 4096, step):
                nc.sync.dma_start(out=raw_bytes[:, lo : lo + step], in_=hb[g][:, half * 4096 + lo : half * 4096 + lo + step])
            bytes_tiles[g, half] = raw_bytes

        def load_raw(u, half):
            at = RAW_AT[u, half]
            raw = space.tile([P, HALF, T * Q], BF16, name="raw%d" % at, offset=at)
            for s in range(0, HALF, 32):
                nc.sync.dma_start(out=raw[:, s : s + 32, :], in_=wv[u][:, half * HALF + s : half * HALF + s + 32, :])
            raws[u, half] = raw

        def widen(copy, g, half, lo, hi):
            if g not in wides:
                wides[g] = space.tile([P, C * PIX], BF16, name="wide%d" % (g % 2), offset=WIDE_AT[g % 2])
            copy(out=wides[g][:, half * 4096 + lo : half * 4096 + hi], in_=bytes_tiles[g, half][:, lo:hi].bitcast(FP8))

        def h_turn(s, y):
            g, word = s // 4, 2 * (s % 4) + y
            turned = psum_h.tile([P, T, P], F32, name="turned")
            for t in range(T):
                nc.tensor.transpose(turned[:, t, :], wides[g][:].bitcast(F32)[:, t * PIX // 2 + word :: T * PIX // 2], ident_f[:])
            groups["turned", s, y] = turned

        def h_scale_step(s):
            grouped = h_tile([P, 4, P, T], BF16)
            for y in range(2):
                nc.vector.tensor_tensor(
                    out=grouped[:, 2 * y : 2 * y + 2],
                    in0=groups["turned", s, y][:].bitcast(BF16).rearrange("p t (n z) -> p z n t", z=2),
                    in1=scale_b,
                    op=ALU.mult,
                )
            groups["h", s] = grouped

        def h_quantise(s):
            g, x = s // 4, 4 * (s % 4)
            for y in range(4):
                nc.vector.quantize_mx(
                    out=h_codes[:, x + y, g * P : (g + 1) * P].bitcast(FP8X4),
                    scales=h_scales[:, x + y, g * P : (g + 1) * P],
                    in_=groups["h", s][:, y].rearrange("p n t -> p (n t)"),
                )

        def regroup(copy, u, k, half, lo=0, hi=HALF):
            if (u, k) not in groups:
                groups[u, k] = unit_tile(u, k)
            (k0, q0), (k3, q3) = unit_list(u)[k][0], unit_list(u)[k][3]
            dst = groups[u, k][:, :, half * HALF + lo : half * HALF + hi, :]
            if k0 == k3:
                copy(
                    out=dst.rearrange("p q m t -> p (m t) q"),
                    in_=raws[u, half][:, lo:hi].rearrange("p m (t q) -> p (m t) q", t=T)[:, :, POS * k0 : POS * k0 + POS],
                )
            else:
                copy(
                    out=dst.rearrange("p (k j) m t -> p (m t) k j", j=2),
                    in_=raws[u, half][:, lo:hi].rearrange("p m (t k i j) -> p (m t) k i j", t=T, i=2, j=2)[:, :, k0 : k0 + 2, q0 // 2, :],
                )

        def regroup_on_gpsimd(u, k, half):
            if (u, k) not in groups:
                groups[u, k] = unit_tile(u, k)
            nc.gpsimd.tensor_scalar(
                out=groups[u, k][:, :, half * HALF : (half + 1) * HALF, :].rearrange("p q m t -> p m q t"),
                in0=raws[u, half][:].rearrange("p m (t q) -> p m q t", t=T)[:, :, POS * k : POS * k + POS, :],
                scalar1=tokens[0][:],
                scalar2=0.0,
                op0=ALU.mult,
                op1=ALU.add,
            )

        def w_quantise(u, k):
            if u not in w_codes:
                at = CODES_AT[u]
                w_codes[u] = space.tile([P, KK, POS, P], U32, align_bytes=64, name="w_codes%d" % at, offset=at)
                w_scales[u] = space.tile([P, KK, POS, P], U8, align_bytes=64, name="w_scales%d" % at, offset=at + 18432)
            nc.vector.quantize_mx(
                out=w_codes[u][:, k].rearrange("p q m -> p (q m)").bitcast(FP8X4),
                scales=w_scales[u][:, k].rearrange("p q m -> p (q m)"),
                in_=groups[u, k][:].rearrange("p q m t -> p (q m t)"),
            )

        def products(u, n, lo, hi, runs=tuple(range(KK)), wanted=(0, 1, 2, 3)):
            for c, (k, q) in enumerate(unit_list(u)[n]):
                if q not in wanted:
                    continue
                order = [kk for r in runs for kk, qq in unit_list(u)[r] if qq == q]
                if (u, q) not in accs:
                    if u % 2:
                        accs[u, q] = psum_h.tile([P, NB], F32, name="turned")
                    else:
                        accs[u, q] = psum_a.tile([P, NB], F32, name="acc")
                i, j = q // 2, q % 2
                pix = (k // 3 + i) * 4 + k % 3 + j
                nc.tensor.matmul_mx(
                    out=accs[u, q][:, lo:hi],
                    lhsT=w_codes[u][:, n, c, :].bitcast(FP8X4),
                    lhsT_scale=w_scales[u][:, n, c, :],
                    rhs=h_codes[:, pix, lo:hi].bitcast(FP8X4),
                    rhs_scale=h_scales[:, pix, lo:hi],
                    start=(k == order[0]),
                    stop=(k == order[-1]),
                )

        def pool_max(u, q):
            b = bias[:, POS * u + q : POS * u + q + 1]
            old = best.get(u)
            if q < POS - 1:
                best[u] = max_pool.tile([P, NB], F32, name="best")
            if q == 0:
                nc.scalar.activation(best[u][:], accs[u, q][:], ACT.Relu, bias=b)
            else:
                dst = best[u][:] if q < POS - 1 else pooled[:, u, :]
                nc.vector.scalar_tensor_tensor(out=dst, in0=accs[u, q][:], scalar=b, in1=old[:], op0=ALU.add, op1=ALU.max)

        load_h(0, 0)
        load_h(0, 1)
        nc.sync.dma_start(out=scale[:], in_=h_scale.rearrange("o (p t) a b -> p (o t a b)", t=T))
        load_h(1, 0)
        load_h(1, 1)
        load_raw(0, 0)
        widen(nc.vector.tensor_copy, 0, 0, 0, 2048)
        widen(nc.scalar.copy, 0, 0, 2048, 4096)
        widen(nc.vector.tensor_copy, 0, 1, 0, 4096)
        load_h(2, 0)
        load_h(2, 1)
        load_raw(0, 1)
        for half in range(2):
            widen(nc.scalar.copy, 1, half, 0, 4096)
        load_h(3, 0)
        load_h(3, 1)
        load_raw(1, 0)
        load_raw(1, 1)
        nc.sync.dma_start(out=bias[:], in_=b2.rearrange("(p u) i j -> p (u i j)", u=U))

        units = [(u, k) for u in range(1, U) for k in range(KK)]
        h_turn(0, 0)
        h_turn(0, 1)
        on_scalar = {
            3: (2,),
            7: (3,),
            11: ((0, 8, 0), (0, 8, 1)),
            12: ((0, 7, 0), (0, 7, 1)),
            13: ((0, 6, 0), (0, 6, 1), (0, 5, 0), (0, 5, 1)),
            14: ((1, 0, 0), (1, 1, 0), (1, 0, 1), (1, 1, 1)),
            15: ((1, 2, 0), (1, 2, 1)),
        }
        quantise = {9: ((0, 0),), 10: ((0, 1),), 11: ((0, 2),), 12: ((0, 3), (0, 8)), 13: ((0, 4), (0, 7)), 14: ((0, 6),), 15: ((0, 5), (1, 0))}
        on_gpsimd = {3: (0, 0), 4: (1, 0), 5: (2, 0), 6: (3, 0), 7: (4, 0), 8: (0, 1), 9: (1, 1), 10: (2, 1), 11: (3, 1), 12: (4, 1)}
        first = (0, 1, 2, 3, 8, 4, 7, 6, 5)
        for s in range(16):
            for job in on_scalar.get(s, ()):
                if job in (2, 3):
                    for half in range(2):
                        widen(nc.scalar.copy, job, half, 0, 4096)
                else:
                    regroup(nc.scalar.copy, *job)
            for n in range(2):
                if s < 15:
                    h_turn(s + 1, n)
            if s in on_gpsimd:
                tokens[0] = token_pool.tile([P, 1], F32, name="token")
                nc.vector.memset(tokens[0][:], 1.0)
                regroup_on_gpsimd(0, *on_gpsimd[s])
            h_scale_step(s)
            if s > 0:
                h_quantise(s - 1)
            for u, k in quantise.get(s, ()):
                w_quantise(u, k)
                if u == 0:
                    products(0, k, 0, 256, first)
        h_quantise(15)
        load_raw(2, 0)
        load_raw(2, 1)
        load_raw(3, 0)
        load_raw(3, 1)

        for k in first:
            products(0, k, 256, 512, first)
        quantised = [(u, k) for s in quantise for u, k in quantise[s] if u > 0]
        for u, k in quantised:
            products(u, k, 0, NB)
        scalar_did = [job for s in on_scalar for job in on_scalar[s] if job not in (2, 3)]
        max_at = {7: (0, 0), 8: (0, 1), 9: (0, 2), 10: (0, 3), 14: (1, 0), 15: (1, 1), 16: (1, 2), 17: (1, 3)}
        for n, (u, k) in enumerate(units[: 2 * KK]):
            for half in range(2):
                if (u, k, half) not in scalar_did:
                    on_vector = half == 1 and n not in ()
                    regroup(nc.vector.tensor_copy if on_vector else nc.scalar.copy, u, k, half)
            if n > 0 and units[n - 1] not in quantised:
                w_quantise(*units[n - 1])
                products(*units[n - 1], 0, NB)
            if n in max_at:
                pool_max(*max_at[n])

        fc_raw = w_tile([P, T, F], BF16)
        nc.sync.dma_start(out=fc_raw[:], in_=fc1_w.rearrange("(p t) f -> p t f", t=T))
        nc.sync.dma_start(out=fc_bias[:], in_=fc1_b.partition_broadcast(P))
        last = U - 1
        for k in (0, 1):
            regroup(nc.scalar.copy, last, k, 0)
        w_quantise(*units[2 * KK - 1])
        products(*units[2 * KK - 1], 0, NB)
        pool_max(last - 1, 0)
        for k in (2, 3):
            regroup(nc.scalar.copy, last, k, 0)
        for k in (4, 5, 6, 7, 8):
            regroup(nc.vector.tensor_copy, last, k, 0)
        for q in range(1, POS):
            pool_max(last - 1, q)
        for k in range(KK):
            regroup(nc.vector.tensor_copy if k in (0, 1) else nc.scalar.copy, last, k, 1, 0, 32)
        warm = psum_a.tile([P, 3 * P], F32, name="acc")
        for k in (2, 3, 4, 0, 1):
            nc.tensor.matmul(
                warm[:],
                lhsT=groups[last, k][:, 0, :32].rearrange("p m t -> p (m t)"),
                rhs=groups[last, k][:, 1, : HALF + 32].rearrange("p m t -> p (m t)"),
                start=True,
                stop=True,
            )
        for k in range(KK):
            regroup(nc.vector.tensor_copy if k in (0, 1) else nc.scalar.copy, last, k, 1, 32, 64)
            w_quantise(last, k)
            products(last, k, 0, NB, wanted=(0, 1, 2))
        for lo in (0, 256):
            for k in range(KK):
                products(last, k, lo, lo + 256, wanted=(3,))
        pool_max(last, 0)
        fc_grouped = w_tile([P, F, T], BF16)
        nc.scalar.copy(out=fc_grouped[:], in_=fc_raw[:].rearrange("p t f -> p f t"))
        pool_max(last, 1)
        pool_max(last, 2)
        nc.vector.quantize_mx(out=fc_codes[:].bitcast(FP8X4), scales=fc_scales[:], in_=fc_grouped[:].rearrange("p f t -> p (f t)"))
        g_codes = space.tile([P, NB], U32, align_bytes=64, name="g_codes", offset=RAW_AT[1, 0])
        g_scales = space.tile([P, NB], U8, align_bytes=64, name="g_scales", offset=RAW_AT[1, 0] + 2048)
        g_grouped = h_tile([P, NB, U], BF16)

        def dense_group(copy, g):
            cols = slice(g * P, (g + 1) * P)
            copy(out=g_grouped[:, cols, :], in_=pooled[:, :, cols].rearrange("p u n -> p n u"))

        def dense_quantise(g):
            cols = slice(g * P, (g + 1) * P)
            nc.vector.quantize_mx(
                out=g_codes[:, cols].bitcast(FP8X4), scales=g_scales[:, cols], in_=g_grouped[:, cols, :].rearrange("p n u -> p (n u)")
            )

        prods = {}

        def dense_product(g):
            cols = slice(g * P, (g + 1) * P)
            prods[g] = psum_a.tile([P, F], F32, name="acc")
            nc.tensor.matmul_mx(
                out=prods[g][:],
                lhsT=g_codes[:, cols].bitcast(FP8X4),
                lhsT_scale=g_scales[:, cols],
                rhs=fc_codes[:].bitcast(FP8X4),
                rhs_scale=fc_scales[:],
                start=True,
                stop=True,
            )

        def dense_out(g):
            cols = slice(g * P, (g + 1) * P)
            total = (h_tile if g == 3 else w_tile)([P, F], F32)
            nc.vector.tensor_tensor(out=total[:], in0=prods[g][:], in1=fc_bias[:], op=ALU.add)
            nc.scalar.activation(total[:], total[:], ACT.Relu)
            nc.sync.dma_start(out=out[cols, :], in_=total[:])

        def last_max(lo):
            nc.vector.scalar_tensor_tensor(
                out=pooled[:, U - 1, lo : lo + 256],
                in0=accs[U - 1, 3][:, lo : lo + 256],
                scalar=bias[:, POS * U - 1 : POS * U],
                in1=best[U - 1][:, lo : lo + 256],
                op0=ALU.add,
                op1=ALU.max,
            )

        last_max(0)
        dense_group(nc.scalar.copy, 1)
        dense_group(nc.vector.tensor_copy, 0)
        dense_quantise(0)
        dense_product(0)
        dense_quantise(1)
        dense_product(1)
        last_max(256)
        dense_group(nc.scalar.copy, 3)
        dense_group(nc.vector.tensor_copy, 2)
        dense_out(0)
        dense_quantise(2)
        dense_product(2)
        dense_quantise(3)
        dense_product(3)
        dense_out(1)
        dense_out(2)
        dense_out(3)
